import numpy as np
import ml_dtypes


def mxq(x, axis, fmt="e4m3"):
    dtype, down = {"e4m3": (ml_dtypes.float8_e4m3fn, 7), "e5m2": (ml_dtypes.float8_e5m2, 14)}[fmt]
    v = np.moveaxis(np.asarray(x, np.float32).astype(ml_dtypes.bfloat16).astype(np.float64), axis, -1)
    blocks = v.reshape(v.shape[:-1] + (-1, 32))
    amax = np.abs(blocks).max(-1, keepdims=True)
    byte = np.maximum(np.where(amax > 0, np.frexp(amax)[1] - 1 + 127, 0) - down, 1)
    scale = np.exp2(byte - 127.0)
    codes = (blocks / scale).astype(np.float32).astype(dtype).astype(np.float64)
    return np.moveaxis((codes * scale).reshape(v.shape), -1, axis)


WIDE = False


def mx_kscale(k):
    if not WIDE:
        return np.ones(k)
    levels = np.array([10, -10, 5, -5, 0])
    a = np.random.permutation(np.resize(levels, k // 512 * 4)).reshape(k // 512, 4)
    idx = np.arange(k)
    return np.exp2(a[idx // 512, idx % 128 // 32])


BF16 = ml_dtypes.bfloat16


def bf(x):
    return np.asarray(x, np.float32).astype(BF16)


def f64(x):
    return np.asarray(x).astype(np.float64)


B, D, HID, G0, RIN, NR = 128, 512, 1024, 512, 256, 5
EPS = 1e-05
W2S = 0.02


def silu(v):
    return v / (1.0 + np.exp(-v))


def setup_inputs():
    s, t = mx_kscale(G0), mx_kscale(HID)
    return {"x0": bf(np.random.standard_normal((B, G0)) * s),
            "w1_g0": bf(np.random.standard_normal((HID, G0)) / np.sqrt(G0) / s),
            "w3_g0": bf(np.random.standard_normal((HID, G0)) / np.sqrt(G0) / s * t[:, None]),
            "w2_g0": bf(np.random.standard_normal((D, HID)) * W2S / np.sqrt(HID) / t),
            "norm_w": bf(1.0 + 0.1 * np.random.standard_normal(D)),
            "norm_b": bf(0.1 * np.random.standard_normal(D)),
            "term_embed0": bf(np.random.standard_normal(D))}


def reference(x0, w1_g0, w3_g0, w2_g0, norm_w, norm_b, term_embed0):
    xq = mxq(f64(x0), 1, "e4m3")
    gate0 = silu(xq @ mxq(f64(w1_g0), 1, "e4m3").T)
    h = gate0 * (xq @ mxq(f64(w3_g0), 1, "e4m3").T)
    tok = mxq(h, 1, "e4m3") @ mxq(f64(w2_g0), 1, "e4m3").T
    rms = np.sqrt(np.mean(tok * tok, axis=-1, keepdims=True) + EPS)
    return (tok / rms) * f64(norm_w) + f64(norm_b) + f64(term_embed0)

@@ -1,0 +1,184 @@
+from contextlib import ExitStack
+
+import concourse.mybir as mybir
+from concourse.masks import make_identity
+
+F32 = mybir.dt.float32
+BF16 = mybir.dt.bfloat16
+I32 = mybir.dt.int32
+U32 = mybir.dt.uint32
+U8 = mybir.dt.uint8
+FP8X4 = mybir.dt.float8_e4m3fn_x4
+ACT = mybir.ActivationFunctionType
+ALU = mybir.AluOpType
+
+P = 128
+PACK = 4
+K_PASS = P * PACK
+PAIRS = K_PASS // 2
+HID = 1024
+D = 512
+EPS = 1e-5
+CHUNKS = 4
+PASSES = HID // K_PASS
+HALF = D // 2
+
+FLOPS = 2 * P * K_PASS * HID * 2 + 2 * P * HID * D
+
+
+def new_piece(pool, name, slabs):
+    return {
+        "slabs": slabs,
+        "raw": pool.tile([P, slabs * K_PASS], BF16, name=name + "_raw"),
+        "grouped": pool.tile([P, slabs * K_PASS], BF16, name=name + "_grouped", align_bytes=64),
+        "codes": pool.tile([P, slabs * P], U32, name=name + "_codes", align_bytes=64),
+        "scales": pool.tile([P, slabs * P], U8, name=name + "_scales", align_bytes=64),
+    }
+
+
+def transpose_piece(nc, banks, piece, identity):
+    words = piece["raw"][:].bitcast(F32)
+    flipped = banks.tile([P, 2 * PAIRS], F32, name="flipped", tag="flipped")
+    for block in range(2 * piece["slabs"]):
+        cols = slice(block * P, (block + 1) * P)
+        nc.tensor.transpose(flipped[:, cols], words[:, cols], identity[:])
+    return flipped
+
+
+def regroup_piece(copy, piece, flipped):
+    slabs = piece["slabs"]
+    copy(
+        out=piece["grouped"][:].bitcast(F32).rearrange("p (s i u) -> p s i u", s=slabs, u=2),
+        in_=flipped[:, 0 : slabs * PAIRS].rearrange("p (s u i) -> p s i u", s=slabs, u=2),
+    )
+
+
+def quantise(nc, codes, scales, grouped):
+    nc.vector.quantize_mx(out=codes[:].bitcast(FP8X4), scales=scales[:], in_=grouped[:])
+
+
+def tile_observationembeddingv2_pa_s_kernel(
+    tc, x0, w1_g0, w3_g0, w2_g0, norm_w, norm_b, term_embed0, out
+):
+    nc = tc.nc
+    with ExitStack() as ctx:
+        keep = ctx.enter_context(tc.tile_pool(name="keep", bufs=1))
+        flip_banks = ctx.enter_context(tc.psum_pool(name="flip_banks", bufs=4))
+        sum_banks = ctx.enter_context(tc.psum_pool(name="sum_banks", bufs=1))
+
+        x_piece = new_piece(keep, "x", 1)
+        w1_pieces = [new_piece(keep, "w1_%d" % c, 2) for c in range(CHUNKS)]
+        w3_pieces = [new_piece(keep, "w3_%d" % c, 2) for c in range(CHUNKS)]
+        w2_pieces = [new_piece(keep, "w2_%d" % d, 2) for d in range(CHUNKS)]
+        nc.sync.dma_start(out=x_piece["raw"][:], in_=x0)
+        w1_rows = w1_g0.rearrange("(c i e) k -> c i (e k)", i=P, e=2)
+        w3_rows = w3_g0.rearrange("(c i e) k -> c i (e k)", i=P, e=2)
+        for c in range(CHUNKS):
+            nc.sync.dma_start(out=w1_pieces[c]["raw"][:], in_=w1_rows[c])
+            nc.sync.dma_start(out=w3_pieces[c]["raw"][:], in_=w3_rows[c])
+        w2_rows = w2_g0.rearrange("(d i) k -> d i k", i=P)
+        for d in range(CHUNKS):
+            nc.sync.dma_start(out=w2_pieces[d]["raw"][:], in_=w2_rows[d])
+
+        identity = keep.tile([P, P], F32, name="identity")
+        make_identity(nc, identity[:])
+        neg_half = keep.tile([P, 1], F32, name="neg_half")
+        nc.gpsimd.memset(neg_half[:], -0.5)
+        ones = keep.tile([P, P], BF16, name="ones")
+        nc.vector.memset(ones[:], 1.0)
+        rows = keep.tile([P, 2 * D], BF16, name="rows")
+        nc.vector.memset(rows[:].bitcast(I32), 0)
+        nc.scalar.dma_start(out=rows[0:1, 0:D], in_=norm_w.rearrange("(o d) -> o d", o=1))
+        nc.scalar.dma_start(out=rows[0:1, D : 2 * D], in_=norm_b.rearrange("(o d) -> o d", o=1))
+        nc.scalar.dma_start(out=rows[1:2, D : 2 * D], in_=term_embed0.rearrange("(o d) -> o d", o=1))
+        warm = keep.tile([P, 1], F32, name="warm")
+        nc.scalar.activation(out=warm[:], in_=neg_half[:], func=ACT.Silu)
+
+        def prepare(piece, copy):
+            flipped = transpose_piece(nc, flip_banks, piece, identity)
+            regroup_piece(copy, piece, flipped)
+            quantise(nc, piece["codes"], piece["scales"], piece["grouped"])
+
+        prepare(x_piece, nc.scalar.copy)
+
+        gain_bank = flip_banks.tile([P, D], F32, name="gain_bank", tag="flipped")
+        nc.tensor.matmul(out=gain_bank[:], lhsT=ones[:], rhs=rows[:, 0:D], start=True, stop=True)
+        gain = keep.tile([P, D], F32, name="gain")
+        nc.vector.tensor_copy(out=gain[:], in_=gain_bank[:])
+        shift = sum_banks.tile([P, D], F32, name="shift")
+        nc.tensor.matmul(out=shift[:], lhsT=ones[:], rhs=rows[:, D : 2 * D], start=True, stop=True)
+
+        h_codes = []
+        h_scales = []
+        for g in range(PASSES):
+            for u in range(2):
+                c = 2 * g + u
+                prepare(w1_pieces[c], nc.scalar.copy)
+                prepare(w3_pieces[c], nc.scalar.copy if u == 0 else nc.vector.tensor_copy)
+            gate = sum_banks.tile([P, PACK, P], F32, name="gate_%d" % g, tag="left")
+            up = sum_banks.tile([P, PACK, P], F32, name="up_%d" % g, tag="right")
+            for u in range(2):
+                for e in range(2):
+                    for pieces, bank in ((w1_pieces, gate), (w3_pieces, up)):
+                        nc.tensor.matmul_mx(
+                            out=bank[:, 2 * u + e, :],
+                            lhsT=pieces[2 * g + u]["codes"][:, e * P : (e + 1) * P].bitcast(FP8X4),
+                            lhsT_scale=pieces[2 * g + u]["scales"][:, e * P : (e + 1) * P],
+                            rhs=x_piece["codes"][:].bitcast(FP8X4),
+                            rhs_scale=x_piece["scales"][:],
+                            start=True,
+                            stop=True,
+                        )
+            silu_gate = keep.tile([P, PACK, P], F32, name="silu_gate_%d" % g)
+            nc.scalar.activation(out=silu_gate[:], in_=gate[:], func=ACT.Silu)
+            h_grouped = keep.tile([P, P, PACK], BF16, name="h_grouped_%d" % g, align_bytes=64)
+            nc.vector.tensor_tensor(
+                out=h_grouped[:],
+                in0=silu_gate[:].rearrange("p t b -> p b t"),
+                in1=up[:].rearrange("p t b -> p b t"),
+                op=ALU.mult,
+            )
+            h_codes.append(keep.tile([P, P], U32, name="h_codes_%d" % g, align_bytes=64))
+            h_scales.append(keep.tile([P, P], U8, name="h_scales_%d" % g, align_bytes=64))
+            quantise(nc, h_codes[g], h_scales[g], h_grouped[:].rearrange("p b t -> p (b t)"))
+
+        mean_sq = []
+        scaled = []
+        for j in range(2):
+            tok = sum_banks.tile([P, HALF], F32, name="tok_%d" % j, tag=("left", "right")[j])
+            for n in range(2):
+                piece = w2_pieces[2 * j + n]
+                prepare(piece, nc.scalar.copy)
+                for g in range(PASSES):
+                    nc.tensor.matmul_mx(
+                        out=tok[:, n * P : (n + 1) * P],
+                        lhsT=h_codes[g][:].bitcast(FP8X4),
+                        lhsT_scale=h_scales[g][:],
+                        rhs=piece["codes"][:, g * P : (g + 1) * P].bitcast(FP8X4),
+                        rhs_scale=piece["scales"][:, g * P : (g + 1) * P],
+                        start=(g == 0),
+                        stop=(g == PASSES - 1),
+                    )
+            squares = keep.tile([P, HALF], F32, name="squares_%d" % j)
+            mean_sq.append(keep.tile([P, 1], F32, name="mean_sq_%d" % j))
+            nc.scalar.activation(
+                out=squares[:], in_=tok[:], func=ACT.Square, scale=D**-0.5, accum_out=mean_sq[j][:]
+            )
+            scaled.append(keep.tile([P, HALF], F32, name="scaled_%d" % j))
+            nc.vector.tensor_tensor(
+                out=scaled[j][:], in0=tok[:], in1=gain[:, j * HALF : (j + 1) * HALF], op=ALU.mult
+            )
+
+        mean_eps = keep.tile([P, 1], F32, name="mean_eps")
+        nc.vector.tensor_scalar(
+            out=mean_eps[:], in0=mean_sq[1][:], scalar1=mean_sq[0][:, 0:1], scalar2=EPS, op0=ALU.add, op1=ALU.add
+        )
+        inv_rms = keep.tile([P, 1], F32, name="inv_rms")
+        nc.gpsimd.tensor_tensor(out=inv_rms[:], in0=mean_eps[:], in1=neg_half[:], op=ALU.pow)
+        for j in range(2):
+            cols = slice(j * HALF, (j + 1) * HALF)
+            result = keep.tile([P, HALF], F32, name="result_%d" % j)
+            nc.vector.scalar_tensor_tensor(
+                out=result[:], in0=scaled[j][:], scalar=inv_rms[:, 0:1], in1=shift[:, cols], op0=ALU.mult, op1=ALU.add
+            )
+            nc.sync.dma_start(out=out[:, cols], in_=result[:])

@@ -31,30 +31,42 @@ def new_piece(pool, name, slabs):
         "slabs": slabs,
         "raw": pool.tile([P, slabs * K_PASS], BF16, name=name + "_raw"),
         "grouped": pool.tile([P, slabs * K_PASS], BF16, name=name + "_grouped", align_bytes=64),
-        "codes": pool.tile([P, slabs * P], U32, name=name + "_codes", align_bytes=64),
-        "scales": pool.tile([P, slabs * P], U8, name=name + "_scales", align_bytes=64),
     }
 
 
-def transpose_piece(nc, banks, piece, identity):
+def own_codes(pool, name, piece):
+    codes = pool.tile([P, piece["slabs"] * P], U32, name=name + "_codes", align_bytes=64)
+    scales = pool.tile([P, piece["slabs"] * P], U8, name=name + "_scales", align_bytes=64)
+    piece["codes"] = [codes[:]]
+    piece["scales"] = [scales[:]]
+
+
+def flip(nc, banks, piece, identity):
     words = piece["raw"][:].bitcast(F32)
     flipped = banks.tile([P, 2 * PAIRS], F32, name="flipped", tag="flipped")
     for block in range(2 * piece["slabs"]):
         cols = slice(block * P, (block + 1) * P)
         nc.tensor.transpose(flipped[:, cols], words[:, cols], identity[:])
-    return flipped
+    piece["flipped"] = flipped
 
 
-def regroup_piece(copy, piece, flipped):
+def regroup(copy, piece):
     slabs = piece["slabs"]
     copy(
         out=piece["grouped"][:].bitcast(F32).rearrange("p (s i u) -> p s i u", s=slabs, u=2),
-        in_=flipped[:, 0 : slabs * PAIRS].rearrange("p (s u i) -> p s i u", s=slabs, u=2),
+        in_=piece["flipped"][:, 0 : slabs * PAIRS].rearrange("p (s u i) -> p s i u", s=slabs, u=2),
     )
 
 
-def quantise(nc, codes, scales, grouped):
-    nc.vector.quantize_mx(out=codes[:].bitcast(FP8X4), scales=scales[:], in_=grouped[:])
+def quantise(nc, piece):
+    calls = len(piece["codes"])
+    width = piece["slabs"] * K_PASS // calls
+    for q in range(calls):
+        nc.vector.quantize_mx(
+            out=piece["codes"][q].bitcast(FP8X4),
+            scales=piece["scales"][q],
+            in_=piece["grouped"][:, q * width : (q + 1) * width],
+        )
 
 
 def tile_observationembeddingv2_pa_s_kernel(
@@ -63,8 +75,9 @@ def tile_observationembeddingv2_pa_s_kernel(
     nc = tc.nc
     with ExitStack() as ctx:
         keep = ctx.enter_context(tc.tile_pool(name="keep", bufs=1))
-        flip_banks = ctx.enter_context(tc.psum_pool(name="flip_banks", bufs=4))
+        flip_banks = ctx.enter_context(tc.psum_pool(name="flip_banks", bufs=5))
         sum_banks = ctx.enter_context(tc.psum_pool(name="sum_banks", bufs=1))
+        ctx.enter_context(tc.manual_schedule())
 
         x_piece = new_piece(keep, "x", 1)
         w1_pieces = [new_piece(keep, "w1_%d" % c, 2) for c in range(CHUNKS)]
@@ -80,101 +93,138 @@ def tile_observationembeddingv2_pa_s_kernel(
         for d in range(CHUNKS):
             nc.sync.dma_start(out=w2_pieces[d]["raw"][:], in_=w2_rows[d])
 
+        own_codes(keep, "x", x_piece)
+        for c in range(CHUNKS):
+            own_codes(keep, "w1_%d" % c, w1_pieces[c])
+            own_codes(keep, "w3_%d" % c, w3_pieces[c])
+        w2_codes = [keep.tile([P, PASSES, HALF], U32, name="w2_codes_%d" % j, align_bytes=64) for j in range(2)]
+        w2_scales = [keep.tile([P, PASSES, HALF], U8, name="w2_scales_%d" % j, align_bytes=64) for j in range(2)]
+        for d in range(CHUNKS):
+            j, n = divmod(d, 2)
+            w2_pieces[d]["codes"] = [w2_codes[j][:, g, n * P : (n + 1) * P] for g in range(PASSES)]
+            w2_pieces[d]["scales"] = [w2_scales[j][:, g, n * P : (n + 1) * P] for g in range(PASSES)]
+
         identity = keep.tile([P, P], F32, name="identity")
         make_identity(nc, identity[:])
         neg_half = keep.tile([P, 1], F32, name="neg_half")
         nc.gpsimd.memset(neg_half[:], -0.5)
-        ones = keep.tile([P, P], BF16, name="ones")
-        nc.vector.memset(ones[:], 1.0)
         rows = keep.tile([P, 2 * D], BF16, name="rows")
         nc.vector.memset(rows[:].bitcast(I32), 0)
+        ones = keep.tile([P, P], BF16, name="ones")
+        nc.vector.memset(ones[:], 1.0)
         nc.scalar.dma_start(out=rows[0:1, 0:D], in_=norm_w.rearrange("(o d) -> o d", o=1))
         nc.scalar.dma_start(out=rows[0:1, D : 2 * D], in_=norm_b.rearrange("(o d) -> o d", o=1))
         nc.scalar.dma_start(out=rows[1:2, D : 2 * D], in_=term_embed0.rearrange("(o d) -> o d", o=1))
         warm = keep.tile([P, 1], F32, name="warm")
         nc.scalar.activation(out=warm[:], in_=neg_half[:], func=ACT.Silu)
 
-        def prepare(piece, copy):
-            flipped = transpose_piece(nc, flip_banks, piece, identity)
-            regroup_piece(copy, piece, flipped)
-            quantise(nc, piece["codes"], piece["scales"], piece["grouped"])
-
-        prepare(x_piece, nc.scalar.copy)
-
-        gain_bank = flip_banks.tile([P, D], F32, name="gain_bank", tag="flipped")
-        nc.tensor.matmul(out=gain_bank[:], lhsT=ones[:], rhs=rows[:, 0:D], start=True, stop=True)
         gain = keep.tile([P, D], F32, name="gain")
-        nc.vector.tensor_copy(out=gain[:], in_=gain_bank[:])
         shift = sum_banks.tile([P, D], F32, name="shift")
-        nc.tensor.matmul(out=shift[:], lhsT=ones[:], rhs=rows[:, D : 2 * D], start=True, stop=True)
 
-        h_codes = []
-        h_scales = []
-        for g in range(PASSES):
-            for u in range(2):
-                c = 2 * g + u
-                prepare(w1_pieces[c], nc.scalar.copy)
-                prepare(w3_pieces[c], nc.scalar.copy if u == 0 else nc.vector.tensor_copy)
-            gate = sum_banks.tile([P, PACK, P], F32, name="gate_%d" % g, tag="left")
-            up = sum_banks.tile([P, PACK, P], F32, name="up_%d" % g, tag="right")
-            for u in range(2):
-                for e in range(2):
-                    for pieces, bank in ((w1_pieces, gate), (w3_pieces, up)):
+        def broadcast_vectors():
+            gain_bank = flip_banks.tile([P, D], F32, name="gain_bank", tag="flipped")
+            nc.tensor.matmul(out=gain_bank[:], lhsT=ones[:], rhs=rows[:, 0:D], start=True, stop=True)
+            nc.tensor.matmul(out=shift[:], lhsT=ones[:], rhs=rows[:, D : 2 * D], start=True, stop=True)
+            nc.vector.tensor_copy(out=gain[:], in_=gain_bank[:])
+
+        gate = [None] * PASSES
+        up = [None] * PASSES
+        silu_gate = [keep.tile([P, PACK, P], F32, name="silu_gate_%d" % g) for g in range(PASSES)]
+        h_grouped = [keep.tile([P, P, PACK], BF16, name="h_grouped_%d" % g, align_bytes=64) for g in range(PASSES)]
+        h_codes = [keep.tile([P, P], U32, name="h_codes_%d" % g, align_bytes=64) for g in range(PASSES)]
+        h_scales = [keep.tile([P, P], U8, name="h_scales_%d" % g, align_bytes=64) for g in range(PASSES)]
+
+        def first_products(g):
+            gate[g] = sum_banks.tile([P, PACK, P], F32, name="gate_%d" % g, tag="left")
+            up[g] = sum_banks.tile([P, PACK, P], F32, name="up_%d" % g, tag="right")
+            for pieces, bank in ((w1_pieces, gate[g]), (w3_pieces, up[g])):
+                for u in range(2):
+                    for e in range(2):
                         nc.tensor.matmul_mx(
                             out=bank[:, 2 * u + e, :],
-                            lhsT=pieces[2 * g + u]["codes"][:, e * P : (e + 1) * P].bitcast(FP8X4),
-                            lhsT_scale=pieces[2 * g + u]["scales"][:, e * P : (e + 1) * P],
-                            rhs=x_piece["codes"][:].bitcast(FP8X4),
-                            rhs_scale=x_piece["scales"][:],
+                            lhsT=pieces[2 * g + u]["codes"][0][:, e * P : (e + 1) * P].bitcast(FP8X4),
+                            lhsT_scale=pieces[2 * g + u]["scales"][0][:, e * P : (e + 1) * P],
+                            rhs=x_piece["codes"][0].bitcast(FP8X4),
+                            rhs_scale=x_piece["scales"][0],
                             start=True,
                             stop=True,
                         )
-            silu_gate = keep.tile([P, PACK, P], F32, name="silu_gate_%d" % g)
-            nc.scalar.activation(out=silu_gate[:], in_=gate[:], func=ACT.Silu)
-            h_grouped = keep.tile([P, P, PACK], BF16, name="h_grouped_%d" % g, align_bytes=64)
+            nc.scalar.activation(out=silu_gate[g][:], in_=gate[g][:], func=ACT.Silu)
+
+        def hidden(g):
             nc.vector.tensor_tensor(
-                out=h_grouped[:],
-                in0=silu_gate[:].rearrange("p t b -> p b t"),
-                in1=up[:].rearrange("p t b -> p b t"),
+                out=h_grouped[g][:],
+                in0=silu_gate[g][:].rearrange("p t b -> p b t"),
+                in1=up[g][:].rearrange("p t b -> p b t"),
                 op=ALU.mult,
             )
-            h_codes.append(keep.tile([P, P], U32, name="h_codes_%d" % g, align_bytes=64))
-            h_scales.append(keep.tile([P, P], U8, name="h_scales_%d" % g, align_bytes=64))
-            quantise(nc, h_codes[g], h_scales[g], h_grouped[:].rearrange("p b t -> p (b t)"))
 
-        mean_sq = []
-        scaled = []
+        def quantise_hidden(g):
+            nc.vector.quantize_mx(
+                out=h_codes[g][:].bitcast(FP8X4),
+                scales=h_scales[g][:],
+                in_=h_grouped[g][:].rearrange("p b t -> p (b t)"),
+            )
+
+        flip(nc, flip_banks, x_piece, identity)
+        regroup(nc.scalar.copy, x_piece)
+        previous = x_piece
+        rounds = [
+            [w1_pieces[0], w3_pieces[0], w1_pieces[1], w3_pieces[1]],
+            [w1_pieces[2], w3_pieces[2], w1_pieces[3], w3_pieces[3]],
+            w2_pieces,
+        ]
+        for r in range(len(rounds)):
+            for n in range(CHUNKS):
+                piece = rounds[r][n]
+                flip(nc, flip_banks, piece, identity)
+                regroup(nc.vector.tensor_copy if (r < PASSES and n == CHUNKS - 1) else nc.scalar.copy, piece)
+                quantise(nc, previous)
+                previous = piece
+                if r == 0 and n == 1:
+                    broadcast_vectors()
+                if r > 0 and n == 1:
+                    first_products(r - 1)
+                if r > 0 and n == 2:
+                    hidden(r - 1)
+                if r > 0 and n == 3:
+                    quantise_hidden(r - 1)
+        quantise(nc, previous)
+
+        mean_sq = [keep.tile([P, 1], F32, name="mean_sq_%d" % j) for j in range(2)]
+        scaled = [keep.tile([P, HALF], F32, name="scaled_%d" % j) for j in range(2)]
+        mean_eps = keep.tile([P, 1], F32, name="mean_eps")
+        inv_rms = keep.tile([P, 1], F32, name="inv_rms")
         for j in range(2):
             tok = sum_banks.tile([P, HALF], F32, name="tok_%d" % j, tag=("left", "right")[j])
-            for n in range(2):
-                piece = w2_pieces[2 * j + n]
-                prepare(piece, nc.scalar.copy)
-                for g in range(PASSES):
-                    nc.tensor.matmul_mx(
-                        out=tok[:, n * P : (n + 1) * P],
-                        lhsT=h_codes[g][:].bitcast(FP8X4),
-                        lhsT_scale=h_scales[g][:],
-                        rhs=piece["codes"][:, g * P : (g + 1) * P].bitcast(FP8X4),
-                        rhs_scale=piece["scales"][:, g * P : (g + 1) * P],
-                        start=(g == 0),
-                        stop=(g == PASSES - 1),
-                    )
+            for g in range(PASSES):
+                nc.tensor.matmul_mx(
+                    out=tok[:],
+                    lhsT=h_codes[g][:].bitcast(FP8X4),
+                    lhsT_scale=h_scales[g][:],
+                    rhs=w2_codes[j][:, g, :].bitcast(FP8X4),
+                    rhs_scale=w2_scales[j][:, g, :],
+                    start=(g == 0),
+                    stop=(g == PASSES - 1),
+                )
             squares = keep.tile([P, HALF], F32, name="squares_%d" % j)
-            mean_sq.append(keep.tile([P, 1], F32, name="mean_sq_%d" % j))
             nc.scalar.activation(
                 out=squares[:], in_=tok[:], func=ACT.Square, scale=D**-0.5, accum_out=mean_sq[j][:]
             )
-            scaled.append(keep.tile([P, HALF], F32, name="scaled_%d" % j))
+            if j == 1:
+                nc.vector.tensor_scalar(
+                    out=mean_eps[:],
+                    in0=mean_sq[1][:],
+                    scalar1=mean_sq[0][:, 0:1],
+                    scalar2=EPS,
+                    op0=ALU.add,
+                    op1=ALU.add,
+                )
+                nc.gpsimd.tensor_tensor(out=inv_rms[:], in0=mean_eps[:], in1=neg_half[:], op=ALU.pow)
             nc.vector.tensor_tensor(
                 out=scaled[j][:], in0=tok[:], in1=gain[:, j * HALF : (j + 1) * HALF], op=ALU.mult
             )
 
-        mean_eps = keep.tile([P, 1], F32, name="mean_eps")
-        nc.vector.tensor_scalar(
-            out=mean_eps[:], in0=mean_sq[1][:], scalar1=mean_sq[0][:, 0:1], scalar2=EPS, op0=ALU.add, op1=ALU.add
-        )
-        inv_rms = keep.tile([P, 1], F32, name="inv_rms")
-        nc.gpsimd.tensor_tensor(out=inv_rms[:], in0=mean_eps[:], in1=neg_half[:], op=ALU.pow)
         for j in range(2):
             cols = slice(j * HALF, (j + 1) * HALF)
             result = keep.tile([P, HALF], F32, name="result_%d" % j)

@@ -22,6 +22,7 @@ EPS = 1e-5
 CHUNKS = 4
 PASSES = HID // K_PASS
 HALF = D // 2
+WARM_PASSES = 16
 
 FLOPS = 2 * P * K_PASS * HID * 2 + 2 * P * HID * D
 
@@ -103,6 +104,22 @@ def tile_observationembeddingv2_pa_s_kernel(
             j, n = divmod(d, 2)
             w2_pieces[d]["codes"] = [w2_codes[j][:, g, n * P : (n + 1) * P] for g in range(PASSES)]
             w2_pieces[d]["scales"] = [w2_scales[j][:, g, n * P : (n + 1) * P] for g in range(PASSES)]
+
+        idle = {"slabs": 1, "grouped": keep.tile([P, K_PASS], BF16, name="idle_grouped", align_bytes=64)}
+        own_codes(keep, "idle", idle)
+        nc.vector.memset(idle["grouped"][:].bitcast(I32), 0)
+        quantise(nc, idle)
+        idle_bank = flip_banks.tile([P, P], F32, name="idle_bank", tag="flipped")
+        for w in range(WARM_PASSES):
+            nc.tensor.matmul_mx(
+                out=idle_bank[:],
+                lhsT=idle["codes"][0].bitcast(FP8X4),
+                lhsT_scale=idle["scales"][0],
+                rhs=idle["codes"][0].bitcast(FP8X4),
+                rhs_scale=idle["scales"][0],
+                start=True,
+                stop=True,
+            )
 
         identity = keep.tile([P, P], F32, name="identity")
         make_identity(nc, identity[:])

@@ -22,7 +22,7 @@ EPS = 1e-5
 CHUNKS = 4
 PASSES = HID // K_PASS
 HALF = D // 2
-WARM_PASSES = 16
+WARM_PASSES = 11
 
 FLOPS = 2 * P * K_PASS * HID * 2 + 2 * P * HID * D
 
@@ -80,6 +80,13 @@ def tile_observationembeddingv2_pa_s_kernel(
         sum_banks = ctx.enter_context(tc.psum_pool(name="sum_banks", bufs=1))
         ctx.enter_context(tc.manual_schedule())
 
+        neg_half = keep.tile([P, 1], F32, name="neg_half")
+        nc.gpsimd.memset(neg_half[:], -0.5)
+        warm = keep.tile([P, 1], F32, name="warm")
+        nc.scalar.activation(out=warm[:], in_=neg_half[:], func=ACT.Silu)
+        identity = keep.tile([P, P], F32, name="identity")
+        make_identity(nc, identity[:])
+
         x_piece = new_piece(keep, "x", 1)
         w1_pieces = [new_piece(keep, "w1_%d" % c, 2) for c in range(CHUNKS)]
         w3_pieces = [new_piece(keep, "w3_%d" % c, 2) for c in range(CHUNKS)]
@@ -87,9 +94,15 @@ def tile_observationembeddingv2_pa_s_kernel(
         nc.sync.dma_start(out=x_piece["raw"][:], in_=x0)
         w1_rows = w1_g0.rearrange("(c i e) k -> c i (e k)", i=P, e=2)
         w3_rows = w3_g0.rearrange("(c i e) k -> c i (e k)", i=P, e=2)
+        rows = keep.tile([P, 2 * D], BF16, name="rows")
         for c in range(CHUNKS):
             nc.sync.dma_start(out=w1_pieces[c]["raw"][:], in_=w1_rows[c])
             nc.sync.dma_start(out=w3_pieces[c]["raw"][:], in_=w3_rows[c])
+            if c == 0:
+                nc.gpsimd.memset(rows[:].bitcast(F32), 0.0)
+                nc.sync.dma_start(out=rows[0:1, 0:D], in_=norm_w.rearrange("(o d) -> o d", o=1))
+                nc.sync.dma_start(out=rows[0:1, D : 2 * D], in_=norm_b.rearrange("(o d) -> o d", o=1))
+                nc.sync.dma_start(out=rows[1:2, D : 2 * D], in_=term_embed0.rearrange("(o d) -> o d", o=1))
         w2_rows = w2_g0.rearrange("(d i) k -> d i k", i=P)
         for d in range(CHUNKS):
             nc.sync.dma_start(out=w2_pieces[d]["raw"][:], in_=w2_rows[d])
@@ -121,19 +134,8 @@ def tile_observationembeddingv2_pa_s_kernel(
                 stop=True,
             )
 
-        identity = keep.tile([P, P], F32, name="identity")
-        make_identity(nc, identity[:])
-        neg_half = keep.tile([P, 1], F32, name="neg_half")
-        nc.gpsimd.memset(neg_half[:], -0.5)
-        rows = keep.tile([P, 2 * D], BF16, name="rows")
-        nc.vector.memset(rows[:].bitcast(I32), 0)
         ones = keep.tile([P, P], BF16, name="ones")
         nc.vector.memset(ones[:], 1.0)
-        nc.scalar.dma_start(out=rows[0:1, 0:D], in_=norm_w.rearrange("(o d) -> o d", o=1))
-        nc.scalar.dma_start(out=rows[0:1, D : 2 * D], in_=norm_b.rearrange("(o d) -> o d", o=1))
-        nc.scalar.dma_start(out=rows[1:2, D : 2 * D], in_=term_embed0.rearrange("(o d) -> o d", o=1))
-        warm = keep.tile([P, 1], F32, name="warm")
-        nc.scalar.activation(out=warm[:], in_=neg_half[:], func=ACT.Silu)
 
         gain = keep.tile([P, D], F32, name="gain")
         shift = sum_banks.tile([P, D], F32, name="shift")

@@ -95,10 +95,11 @@ def tile_observationembeddingv2_pa_s_kernel(
         w1_rows = w1_g0.rearrange("(c i e) k -> c i (e k)", i=P, e=2)
         w3_rows = w3_g0.rearrange("(c i e) k -> c i (e k)", i=P, e=2)
         rows = keep.tile([P, 2 * D], BF16, name="rows")
-        for c in range(CHUNKS):
-            nc.sync.dma_start(out=w1_pieces[c]["raw"][:], in_=w1_rows[c])
-            nc.sync.dma_start(out=w3_pieces[c]["raw"][:], in_=w3_rows[c])
-            if c == 0:
+        for g in range(PASSES):
+            for pieces, rows_in_hbm in ((w1_pieces, w1_rows), (w3_pieces, w3_rows)):
+                for c in (2 * g, 2 * g + 1):
+                    nc.sync.dma_start(out=pieces[c]["raw"][:], in_=rows_in_hbm[c])
+            if g == 0:
                 nc.gpsimd.memset(rows[:].bitcast(F32), 0.0)
                 nc.sync.dma_start(out=rows[0:1, 0:D], in_=norm_w.rearrange("(o d) -> o d", o=1))
                 nc.sync.dma_start(out=rows[0:1, D : 2 * D], in_=norm_b.rearrange("(o d) -> o d", o=1))
@@ -153,22 +154,27 @@ def tile_observationembeddingv2_pa_s_kernel(
         h_codes = [keep.tile([P, P], U32, name="h_codes_%d" % g, align_bytes=64) for g in range(PASSES)]
         h_scales = [keep.tile([P, P], U8, name="h_scales_%d" % g, align_bytes=64) for g in range(PASSES)]
 
-        def first_products(g):
+        def products(bank, pieces, g):
+            for u in range(2):
+                for e in range(2):
+                    nc.tensor.matmul_mx(
+                        out=bank[:, 2 * u + e, :],
+                        lhsT=pieces[2 * g + u]["codes"][0][:, e * P : (e + 1) * P].bitcast(FP8X4),
+                        lhsT_scale=pieces[2 * g + u]["scales"][0][:, e * P : (e + 1) * P],
+                        rhs=x_piece["codes"][0].bitcast(FP8X4),
+                        rhs_scale=x_piece["scales"][0],
+                        start=True,
+                        stop=True,
+                    )
+
+        def gate_products(g):
             gate[g] = sum_banks.tile([P, PACK, P], F32, name="gate_%d" % g, tag="left")
-            up[g] = sum_banks.tile([P, PACK, P], F32, name="up_%d" % g, tag="right")
-            for pieces, bank in ((w1_pieces, gate[g]), (w3_pieces, up[g])):
-                for u in range(2):
-                    for e in range(2):
-                        nc.tensor.matmul_mx(
-                            out=bank[:, 2 * u + e, :],
-                            lhsT=pieces[2 * g + u]["codes"][0][:, e * P : (e + 1) * P].bitcast(FP8X4),
-                            lhsT_scale=pieces[2 * g + u]["scales"][0][:, e * P : (e + 1) * P],
-                            rhs=x_piece["codes"][0].bitcast(FP8X4),
-                            rhs_scale=x_piece["scales"][0],
-                            start=True,
-                            stop=True,
-                        )
+            products(gate[g], w1_pieces, g)
             nc.scalar.activation(out=silu_gate[g][:], in_=gate[g][:], func=ACT.Silu)
+
+        def up_products(g):
+            up[g] = sum_banks.tile([P, PACK, P], F32, name="up_%d" % g, tag="right")
+            products(up[g], w3_pieces, g)
 
         def hidden(g):
             nc.vector.tensor_tensor(
@@ -185,29 +191,30 @@ def tile_observationembeddingv2_pa_s_kernel(
                 in_=h_grouped[g][:].rearrange("p b t -> p (b t)"),
             )
 
+        line = []
+        for g in range(PASSES):
+            line += w1_pieces[2 * g : 2 * g + 2] + w3_pieces[2 * g : 2 * g + 2]
+        line += w2_pieces
         flip(nc, flip_banks, x_piece, identity)
         regroup(nc.scalar.copy, x_piece)
+        flip(nc, flip_banks, line[0], identity)
         previous = x_piece
-        rounds = [
-            [w1_pieces[0], w3_pieces[0], w1_pieces[1], w3_pieces[1]],
-            [w1_pieces[2], w3_pieces[2], w1_pieces[3], w3_pieces[3]],
-            w2_pieces,
-        ]
-        for r in range(len(rounds)):
-            for n in range(CHUNKS):
-                piece = rounds[r][n]
-                flip(nc, flip_banks, piece, identity)
-                regroup(nc.vector.tensor_copy if (r < PASSES and n == CHUNKS - 1) else nc.scalar.copy, piece)
-                quantise(nc, previous)
-                previous = piece
-                if r == 0 and n == 1:
-                    broadcast_vectors()
-                if r > 0 and n == 1:
-                    first_products(r - 1)
-                if r > 0 and n == 2:
-                    hidden(r - 1)
-                if r > 0 and n == 3:
-                    quantise_hidden(r - 1)
+        for i in range(len(line)):
+            r, n = divmod(i, CHUNKS)
+            if i + 1 < len(line):
+                flip(nc, flip_banks, line[i + 1], identity)
+            regroup(nc.vector.tensor_copy if n == 1 else nc.scalar.copy, line[i])
+            quantise(nc, previous)
+            previous = line[i]
+            if i == 1:
+                broadcast_vectors()
+            if r > 0 and n == 0:
+                gate_products(r - 1)
+            if r > 0 and n == 1:
+                up_products(r - 1)
+                hidden(r - 1)
+            if r > 0 and n == 2:
+                quantise_hidden(r - 1)
         quantise(nc, previous)
 
         mean_sq = [keep.tile([P, 1], F32, name="mean_sq_%d" % j) for j in range(2)]

@@ -21,6 +21,7 @@ D = 512
 EPS = 1e-5
 CHUNKS = 4
 PASSES = HID // K_PASS
+GROUPS = (2 * P, P, P)
 HALF = D // 2
 WARM_PASSES = 11
 
@@ -90,7 +91,8 @@ def tile_observationembeddingv2_pa_s_kernel(
         x_piece = new_piece(keep, "x", 1)
         w1_pieces = [new_piece(keep, "w1_%d" % c, 2) for c in range(CHUNKS)]
         w3_pieces = [new_piece(keep, "w3_%d" % c, 2) for c in range(CHUNKS)]
-        w2_pieces = [new_piece(keep, "w2_%d" % d, 2) for d in range(CHUNKS)]
+        w2_pieces = [new_piece(keep, "w2_%d" % d, PASSES) for d in range(CHUNKS - 1)]
+        w2_pieces += [new_piece(keep, "w2_last_%d" % g, 1) for g in range(PASSES)]
         nc.sync.dma_start(out=x_piece["raw"][:], in_=x0)
         w1_rows = w1_g0.rearrange("(c i e) k -> c i (e k)", i=P, e=2)
         w3_rows = w3_g0.rearrange("(c i e) k -> c i (e k)", i=P, e=2)
@@ -105,19 +107,29 @@ def tile_observationembeddingv2_pa_s_kernel(
                 nc.sync.dma_start(out=rows[0:1, D : 2 * D], in_=norm_b.rearrange("(o d) -> o d", o=1))
                 nc.sync.dma_start(out=rows[1:2, D : 2 * D], in_=term_embed0.rearrange("(o d) -> o d", o=1))
         w2_rows = w2_g0.rearrange("(d i) k -> d i k", i=P)
-        for d in range(CHUNKS):
+        for d in range(CHUNKS - 1):
             nc.sync.dma_start(out=w2_pieces[d]["raw"][:], in_=w2_rows[d])
+        for g in range(PASSES):
+            nc.sync.dma_start(
+                out=w2_pieces[CHUNKS - 1 + g]["raw"][:], in_=w2_rows[CHUNKS - 1][:, g * K_PASS : (g + 1) * K_PASS]
+            )
 
         own_codes(keep, "x", x_piece)
         for c in range(CHUNKS):
             own_codes(keep, "w1_%d" % c, w1_pieces[c])
             own_codes(keep, "w3_%d" % c, w3_pieces[c])
-        w2_codes = [keep.tile([P, PASSES, HALF], U32, name="w2_codes_%d" % j, align_bytes=64) for j in range(2)]
-        w2_scales = [keep.tile([P, PASSES, HALF], U8, name="w2_scales_%d" % j, align_bytes=64) for j in range(2)]
+        w2_codes = [keep.tile([P, PASSES, w], U32, name="w2_codes_%d" % j, align_bytes=64) for j, w in enumerate(GROUPS)]
+        w2_scales = [keep.tile([P, PASSES, w], U8, name="w2_scales_%d" % j, align_bytes=64) for j, w in enumerate(GROUPS)]
+        places = [(0, 0), (0, P), (1, 0), (2, 0)]
         for d in range(CHUNKS):
-            j, n = divmod(d, 2)
-            w2_pieces[d]["codes"] = [w2_codes[j][:, g, n * P : (n + 1) * P] for g in range(PASSES)]
-            w2_pieces[d]["scales"] = [w2_scales[j][:, g, n * P : (n + 1) * P] for g in range(PASSES)]
+            j, first = places[d]
+            codes = [w2_codes[j][:, g, first : first + P] for g in range(PASSES)]
+            scales = [w2_scales[j][:, g, first : first + P] for g in range(PASSES)]
+            if d < CHUNKS - 1:
+                w2_pieces[d]["codes"], w2_pieces[d]["scales"] = codes, scales
+            else:
+                for g in range(PASSES):
+                    w2_pieces[d + g]["codes"], w2_pieces[d + g]["scales"] = codes[g : g + 1], scales[g : g + 1]
 
         idle = {"slabs": 1, "grouped": keep.tile([P, K_PASS], BF16, name="idle_grouped", align_bytes=64)}
         own_codes(keep, "idle", idle)
@@ -208,21 +220,26 @@ def tile_observationembeddingv2_pa_s_kernel(
             previous = line[i]
             if i == 1:
                 broadcast_vectors()
-            if r > 0 and n == 0:
+            if 0 < r <= PASSES and n == 0:
                 gate_products(r - 1)
-            if r > 0 and n == 1:
+            if 0 < r <= PASSES and n == 1:
                 up_products(r - 1)
                 hidden(r - 1)
-            if r > 0 and n == 2:
+            if 0 < r <= PASSES and n == 2:
                 quantise_hidden(r - 1)
         quantise(nc, previous)
 
-        mean_sq = [keep.tile([P, 1], F32, name="mean_sq_%d" % j) for j in range(2)]
-        scaled = [keep.tile([P, HALF], F32, name="scaled_%d" % j) for j in range(2)]
+        mean_sq = [keep.tile([P, 1], F32, name="mean_sq_%d" % j) for j in range(len(GROUPS))]
+        scaled = keep.tile([P, D], F32, name="scaled")
+        partial = keep.tile([P, 1], F32, name="partial")
         mean_eps = keep.tile([P, 1], F32, name="mean_eps")
         inv_rms = keep.tile([P, 1], F32, name="inv_rms")
-        for j in range(2):
-            tok = sum_banks.tile([P, HALF], F32, name="tok_%d" % j, tag=("left", "right")[j])
+        first = 0
+        for j, width in enumerate(GROUPS):
+            if j < 2:
+                tok = sum_banks.tile([P, width], F32, name="tok_%d" % j, tag=("left", "right")[j])
+            else:
+                tok = flip_banks.tile([P, width], F32, name="tok_%d" % j, tag="flipped")
             for g in range(PASSES):
                 nc.tensor.matmul_mx(
                     out=tok[:],
@@ -233,28 +250,35 @@ def tile_observationembeddingv2_pa_s_kernel(
                     start=(g == 0),
                     stop=(g == PASSES - 1),
                 )
-            squares = keep.tile([P, HALF], F32, name="squares_%d" % j)
+            squares = keep.tile([P, width], F32, name="squares_%d" % j)
             nc.scalar.activation(
                 out=squares[:], in_=tok[:], func=ACT.Square, scale=D**-0.5, accum_out=mean_sq[j][:]
             )
             if j == 1:
                 nc.vector.tensor_scalar(
-                    out=mean_eps[:],
+                    out=partial[:],
                     in0=mean_sq[1][:],
                     scalar1=mean_sq[0][:, 0:1],
                     scalar2=EPS,
                     op0=ALU.add,
                     op1=ALU.add,
                 )
+            if j == 2:
+                nc.vector.tensor_tensor(out=mean_eps[:], in0=mean_sq[2][:], in1=partial[:], op=ALU.add)
                 nc.gpsimd.tensor_tensor(out=inv_rms[:], in0=mean_eps[:], in1=neg_half[:], op=ALU.pow)
-            nc.vector.tensor_tensor(
-                out=scaled[j][:], in0=tok[:], in1=gain[:, j * HALF : (j + 1) * HALF], op=ALU.mult
-            )
+            cols = slice(first, first + width)
+            nc.vector.tensor_tensor(out=scaled[:, cols], in0=tok[:], in1=gain[:, cols], op=ALU.mult)
+            first += width
 
         for j in range(2):
             cols = slice(j * HALF, (j + 1) * HALF)
             result = keep.tile([P, HALF], F32, name="result_%d" % j)
             nc.vector.scalar_tensor_tensor(
-                out=result[:], in0=scaled[j][:], scalar=inv_rms[:, 0:1], in1=shift[:, cols], op0=ALU.mult, op1=ALU.add
+                out=result[:],
+                in0=scaled[:, cols],
+                scalar=inv_rms[:, 0:1],
+                in1=shift[:, cols],
+                op0=ALU.mult,
+                op1=ALU.add,
             )
             nc.sync.dma_start(out=out[:, cols], in_=result[:])

@@ -77,7 +77,7 @@ def tile_observationembeddingv2_pa_s_kernel(
     nc = tc.nc
     with ExitStack() as ctx:
         keep = ctx.enter_context(tc.tile_pool(name="keep", bufs=1))
-        flip_banks = ctx.enter_context(tc.psum_pool(name="flip_banks", bufs=5))
+        flip_banks = ctx.enter_context(tc.psum_pool(name="flip_banks", bufs=6))
         sum_banks = ctx.enter_context(tc.psum_pool(name="sum_banks", bufs=1))
         ctx.enter_context(tc.manual_schedule())
 
@@ -151,13 +151,14 @@ def tile_observationembeddingv2_pa_s_kernel(
         nc.vector.memset(ones[:], 1.0)
 
         gain = keep.tile([P, D], F32, name="gain")
-        shift = sum_banks.tile([P, D], F32, name="shift")
 
         def broadcast_vectors():
+            shift = flip_banks.tile([P, D], F32, name="shift", tag="flipped")
             gain_bank = flip_banks.tile([P, D], F32, name="gain_bank", tag="flipped")
             nc.tensor.matmul(out=gain_bank[:], lhsT=ones[:], rhs=rows[:, 0:D], start=True, stop=True)
             nc.tensor.matmul(out=shift[:], lhsT=ones[:], rhs=rows[:, D : 2 * D], start=True, stop=True)
             nc.vector.tensor_copy(out=gain[:], in_=gain_bank[:])
+            return shift
 
         gate = [None] * PASSES
         up = [None] * PASSES
@@ -215,19 +216,18 @@ def tile_observationembeddingv2_pa_s_kernel(
             r, n = divmod(i, CHUNKS)
             if i + 1 < len(line):
                 flip(nc, flip_banks, line[i + 1], identity)
-            regroup(nc.vector.tensor_copy if n == 1 else nc.scalar.copy, line[i])
+            regroup(nc.vector.tensor_copy if (r < PASSES and n == 1) else nc.scalar.copy, line[i])
+            if 0 < r <= PASSES and n == 2:
+                hidden(r - 1)
             quantise(nc, previous)
             previous = line[i]
-            if i == 1:
-                broadcast_vectors()
-            if 0 < r <= PASSES and n == 0:
-                gate_products(r - 1)
-            if 0 < r <= PASSES and n == 1:
-                up_products(r - 1)
-                hidden(r - 1)
             if 0 < r <= PASSES and n == 2:
                 quantise_hidden(r - 1)
+            if 0 < r <= PASSES and n == 0:
+                gate_products(r - 1)
+                up_products(r - 1)
         quantise(nc, previous)
+        shift = broadcast_vectors()
 
         mean_sq = [keep.tile([P, 1], F32, name="mean_sq_%d" % j) for j in range(len(GROUPS))]
         scaled = keep.tile([P, D], F32, name="scaled")

@@ -234,12 +234,13 @@ def tile_observationembeddingv2_pa_s_kernel(
         partial = keep.tile([P, 1], F32, name="partial")
         mean_eps = keep.tile([P, 1], F32, name="mean_eps")
         inv_rms = keep.tile([P, 1], F32, name="inv_rms")
-        first = 0
+        toks = []
         for j, width in enumerate(GROUPS):
             if j < 2:
                 tok = sum_banks.tile([P, width], F32, name="tok_%d" % j, tag=("left", "right")[j])
             else:
                 tok = flip_banks.tile([P, width], F32, name="tok_%d" % j, tag="flipped")
+            toks.append(tok)
             for g in range(PASSES):
                 nc.tensor.matmul_mx(
                     out=tok[:],
@@ -254,20 +255,20 @@ def tile_observationembeddingv2_pa_s_kernel(
             nc.scalar.activation(
                 out=squares[:], in_=tok[:], func=ACT.Square, scale=D**-0.5, accum_out=mean_sq[j][:]
             )
-            if j == 1:
-                nc.vector.tensor_scalar(
-                    out=partial[:],
-                    in0=mean_sq[1][:],
-                    scalar1=mean_sq[0][:, 0:1],
-                    scalar2=EPS,
-                    op0=ALU.add,
-                    op1=ALU.add,
-                )
-            if j == 2:
-                nc.vector.tensor_tensor(out=mean_eps[:], in0=mean_sq[2][:], in1=partial[:], op=ALU.add)
-                nc.gpsimd.tensor_tensor(out=inv_rms[:], in0=mean_eps[:], in1=neg_half[:], op=ALU.pow)
+        nc.vector.tensor_scalar(
+            out=partial[:],
+            in0=mean_sq[1][:],
+            scalar1=mean_sq[0][:, 0:1],
+            scalar2=EPS,
+            op0=ALU.add,
+            op1=ALU.add,
+        )
+        nc.vector.tensor_tensor(out=mean_eps[:], in0=mean_sq[2][:], in1=partial[:], op=ALU.add)
+        nc.gpsimd.tensor_tensor(out=inv_rms[:], in0=mean_eps[:], in1=neg_half[:], op=ALU.pow)
+        first = 0
+        for j, width in enumerate(GROUPS):
             cols = slice(first, first + width)
-            nc.vector.tensor_tensor(out=scaled[:, cols], in0=tok[:], in1=gain[:, cols], op=ALU.mult)
+            nc.vector.tensor_tensor(out=scaled[:, cols], in0=toks[j][:], in1=gain[:, cols], op=ALU.mult)
             first += width
 
         for j in range(2):

@@ -101,11 +101,6 @@ def tile_observationembeddingv2_pa_s_kernel(
             for pieces, rows_in_hbm in ((w1_pieces, w1_rows), (w3_pieces, w3_rows)):
                 for c in (2 * g, 2 * g + 1):
                     nc.sync.dma_start(out=pieces[c]["raw"][:], in_=rows_in_hbm[c])
-            if g == 0:
-                nc.gpsimd.memset(rows[:].bitcast(F32), 0.0)
-                nc.sync.dma_start(out=rows[0:1, 0:D], in_=norm_w.rearrange("(o d) -> o d", o=1))
-                nc.sync.dma_start(out=rows[0:1, D : 2 * D], in_=norm_b.rearrange("(o d) -> o d", o=1))
-                nc.sync.dma_start(out=rows[1:2, D : 2 * D], in_=term_embed0.rearrange("(o d) -> o d", o=1))
         w2_rows = w2_g0.rearrange("(d i) k -> d i k", i=P)
         for d in range(CHUNKS - 1):
             nc.sync.dma_start(out=w2_pieces[d]["raw"][:], in_=w2_rows[d])
@@ -113,6 +108,10 @@ def tile_observationembeddingv2_pa_s_kernel(
             nc.sync.dma_start(
                 out=w2_pieces[CHUNKS - 1 + g]["raw"][:], in_=w2_rows[CHUNKS - 1][:, g * K_PASS : (g + 1) * K_PASS]
             )
+        nc.gpsimd.memset(rows[:].bitcast(F32), 0.0)
+        nc.sync.dma_start(out=rows[0:1, 0:D], in_=norm_w.rearrange("(o d) -> o d", o=1))
+        nc.sync.dma_start(out=rows[0:1, D : 2 * D], in_=norm_b.rearrange("(o d) -> o d", o=1))
+        nc.sync.dma_start(out=rows[1:2, D : 2 * D], in_=term_embed0.rearrange("(o d) -> o d", o=1))
 
         own_codes(keep, "x", x_piece)
         for c in range(CHUNKS):

@@ -21,8 +21,10 @@ D = 512
 EPS = 1e-5
 CHUNKS = 4
 PASSES = HID // K_PASS
-GROUPS = (2 * P, P, P)
+GROUPS = ((0, 1), (2,), (3,))
 HALF = D // 2
+HIDDEN_STEPS = (7, 10)
+HIDDEN_QUANTISE_STEPS = (8, 10)
 WARM_PASSES = 11
 
 FLOPS = 2 * P * K_PASS * HID * 2 + 2 * P * HID * D
@@ -39,8 +41,8 @@ def new_piece(pool, name, slabs):
 def own_codes(pool, name, piece):
     codes = pool.tile([P, piece["slabs"] * P], U32, name=name + "_codes", align_bytes=64)
     scales = pool.tile([P, piece["slabs"] * P], U8, name=name + "_scales", align_bytes=64)
-    piece["codes"] = [codes[:]]
-    piece["scales"] = [scales[:]]
+    piece["codes"] = codes[:]
+    piece["scales"] = scales[:]
 
 
 def flip(nc, banks, piece, identity):
@@ -61,14 +63,7 @@ def regroup(copy, piece):
 
 
 def quantise(nc, piece):
-    calls = len(piece["codes"])
-    width = piece["slabs"] * K_PASS // calls
-    for q in range(calls):
-        nc.vector.quantize_mx(
-            out=piece["codes"][q].bitcast(FP8X4),
-            scales=piece["scales"][q],
-            in_=piece["grouped"][:, q * width : (q + 1) * width],
-        )
+    nc.vector.quantize_mx(out=piece["codes"].bitcast(FP8X4), scales=piece["scales"], in_=piece["grouped"][:])
 
 
 def tile_observationembeddingv2_pa_s_kernel(
@@ -117,18 +112,13 @@ def tile_observationembeddingv2_pa_s_kernel(
         for c in range(CHUNKS):
             own_codes(keep, "w1_%d" % c, w1_pieces[c])
             own_codes(keep, "w3_%d" % c, w3_pieces[c])
-        w2_codes = [keep.tile([P, PASSES, w], U32, name="w2_codes_%d" % j, align_bytes=64) for j, w in enumerate(GROUPS)]
-        w2_scales = [keep.tile([P, PASSES, w], U8, name="w2_scales_%d" % j, align_bytes=64) for j, w in enumerate(GROUPS)]
-        places = [(0, 0), (0, P), (1, 0), (2, 0)]
-        for d in range(CHUNKS):
-            j, first = places[d]
-            codes = [w2_codes[j][:, g, first : first + P] for g in range(PASSES)]
-            scales = [w2_scales[j][:, g, first : first + P] for g in range(PASSES)]
-            if d < CHUNKS - 1:
-                w2_pieces[d]["codes"], w2_pieces[d]["scales"] = codes, scales
-            else:
-                for g in range(PASSES):
-                    w2_pieces[d + g]["codes"], w2_pieces[d + g]["scales"] = codes[g : g + 1], scales[g : g + 1]
+        w2_words = []
+        for n in range(len(w2_pieces)):
+            own_codes(keep, "w2_%d" % n, w2_pieces[n])
+        for d in range(CHUNKS - 1):
+            codes, scales = w2_pieces[d]["codes"], w2_pieces[d]["scales"]
+            w2_words.append([(codes[:, g * P : (g + 1) * P], scales[:, g * P : (g + 1) * P]) for g in range(PASSES)])
+        w2_words.append([(piece["codes"], piece["scales"]) for piece in w2_pieces[CHUNKS - 1 :]])
 
         idle = {"slabs": 1, "grouped": keep.tile([P, K_PASS], BF16, name="idle_grouped", align_bytes=64)}
         own_codes(keep, "idle", idle)
@@ -138,10 +128,10 @@ def tile_observationembeddingv2_pa_s_kernel(
         for w in range(WARM_PASSES):
             nc.tensor.matmul_mx(
                 out=idle_bank[:],
-                lhsT=idle["codes"][0].bitcast(FP8X4),
-                lhsT_scale=idle["scales"][0],
-                rhs=idle["codes"][0].bitcast(FP8X4),
-                rhs_scale=idle["scales"][0],
+                lhsT=idle["codes"].bitcast(FP8X4),
+                lhsT_scale=idle["scales"],
+                rhs=idle["codes"].bitcast(FP8X4),
+                rhs_scale=idle["scales"],
                 start=True,
                 stop=True,
             )
@@ -171,10 +161,10 @@ def tile_observationembeddingv2_pa_s_kernel(
                 for e in range(2):
                     nc.tensor.matmul_mx(
                         out=bank[:, 2 * u + e, :],
-                        lhsT=pieces[2 * g + u]["codes"][0][:, e * P : (e + 1) * P].bitcast(FP8X4),
-                        lhsT_scale=pieces[2 * g + u]["scales"][0][:, e * P : (e + 1) * P],
-                        rhs=x_piece["codes"][0].bitcast(FP8X4),
-                        rhs_scale=x_piece["scales"][0],
+                        lhsT=pieces[2 * g + u]["codes"][:, e * P : (e + 1) * P].bitcast(FP8X4),
+                        lhsT_scale=pieces[2 * g + u]["scales"][:, e * P : (e + 1) * P],
+                        rhs=x_piece["codes"].bitcast(FP8X4),
+                        rhs_scale=x_piece["scales"],
                         start=True,
                         stop=True,
                     )
@@ -182,6 +172,8 @@ def tile_observationembeddingv2_pa_s_kernel(
         def gate_products(g):
             gate[g] = sum_banks.tile([P, PACK, P], F32, name="gate_%d" % g, tag="left")
             products(gate[g], w1_pieces, g)
+
+        def silu(g):
             nc.scalar.activation(out=silu_gate[g][:], in_=gate[g][:], func=ACT.Silu)
 
         def up_products(g):
@@ -216,14 +208,17 @@ def tile_observationembeddingv2_pa_s_kernel(
             if i + 1 < len(line):
                 flip(nc, flip_banks, line[i + 1], identity)
             regroup(nc.vector.tensor_copy if (r < PASSES and n == 1) else nc.scalar.copy, line[i])
-            if 0 < r <= PASSES and n == 2:
-                hidden(r - 1)
+            if i in HIDDEN_STEPS:
+                hidden(HIDDEN_STEPS.index(i))
             quantise(nc, previous)
             previous = line[i]
-            if 0 < r <= PASSES and n == 2:
-                quantise_hidden(r - 1)
-            if 0 < r <= PASSES and n == 0:
-                gate_products(r - 1)
+            if i in HIDDEN_QUANTISE_STEPS:
+                quantise_hidden(HIDDEN_QUANTISE_STEPS.index(i))
+            if n == 3 and r < PASSES:
+                gate_products(r)
+            if n == 0 and 0 < r <= PASSES:
+                silu(r - 1)
+            if n == 1 and 0 < r <= PASSES:
                 up_products(r - 1)
         quantise(nc, previous)
         shift = broadcast_vectors()
@@ -234,41 +229,44 @@ def tile_observationembeddingv2_pa_s_kernel(
         mean_eps = keep.tile([P, 1], F32, name="mean_eps")
         inv_rms = keep.tile([P, 1], F32, name="inv_rms")
         toks = []
-        for j, width in enumerate(GROUPS):
+        for j, chunks in enumerate(GROUPS):
+            width = len(chunks) * P
             if j < 2:
                 tok = sum_banks.tile([P, width], F32, name="tok_%d" % j, tag=("left", "right")[j])
             else:
                 tok = flip_banks.tile([P, width], F32, name="tok_%d" % j, tag="flipped")
             toks.append(tok)
-            for g in range(PASSES):
-                nc.tensor.matmul_mx(
-                    out=tok[:],
-                    lhsT=h_codes[g][:].bitcast(FP8X4),
-                    lhsT_scale=h_scales[g][:],
-                    rhs=w2_codes[j][:, g, :].bitcast(FP8X4),
-                    rhs_scale=w2_scales[j][:, g, :],
-                    start=(g == 0),
-                    stop=(g == PASSES - 1),
-                )
+            for n, d in enumerate(chunks):
+                for g in range(PASSES):
+                    codes, scales = w2_words[d][g]
+                    nc.tensor.matmul_mx(
+                        out=tok[:, n * P : (n + 1) * P],
+                        lhsT=h_codes[g][:].bitcast(FP8X4),
+                        lhsT_scale=h_scales[g][:],
+                        rhs=codes.bitcast(FP8X4),
+                        rhs_scale=scales,
+                        start=(g == 0),
+                        stop=(g == PASSES - 1),
+                    )
             squares = keep.tile([P, width], F32, name="squares_%d" % j)
             nc.scalar.activation(
                 out=squares[:], in_=tok[:], func=ACT.Square, scale=D**-0.5, accum_out=mean_sq[j][:]
             )
-        nc.vector.tensor_scalar(
-            out=partial[:],
-            in0=mean_sq[1][:],
-            scalar1=mean_sq[0][:, 0:1],
-            scalar2=EPS,
+        nc.vector.tensor_scalar(out=partial[:], in0=mean_sq[0][:], scalar1=EPS, scalar2=None, op0=ALU.add)
+        nc.vector.scalar_tensor_tensor(
+            out=mean_eps[:],
+            in0=mean_sq[2][:],
+            scalar=mean_sq[1][:, 0:1],
+            in1=partial[:],
             op0=ALU.add,
             op1=ALU.add,
         )
-        nc.vector.tensor_tensor(out=mean_eps[:], in0=mean_sq[2][:], in1=partial[:], op=ALU.add)
         nc.gpsimd.tensor_tensor(out=inv_rms[:], in0=mean_eps[:], in1=neg_half[:], op=ALU.pow)
         first = 0
-        for j, width in enumerate(GROUPS):
-            cols = slice(first, first + width)
+        for j, chunks in enumerate(GROUPS):
+            cols = slice(first, first + len(chunks) * P)
             nc.vector.tensor_tensor(out=scaled[:, cols], in0=toks[j][:], in1=gain[:, cols], op=ALU.mult)
-            first += width
+            first += len(chunks) * P
 
         for j in range(2):
             cols = slice(j * HALF, (j + 1) * HALF)

@@ -23,6 +23,8 @@ CHUNKS = 4
 PASSES = HID // K_PASS
 GROUPS = ((0, 1), (2,), (3,))
 HALF = D // 2
+GATE_STEPS = (4, 8)
+UP_STEPS = (5, 8)
 HIDDEN_STEPS = (7, 10)
 HIDDEN_QUANTISE_STEPS = (8, 10)
 WARM_PASSES = 11
@@ -172,8 +174,6 @@ def tile_observationembeddingv2_pa_s_kernel(
         def gate_products(g):
             gate[g] = sum_banks.tile([P, PACK, P], F32, name="gate_%d" % g, tag="left")
             products(gate[g], w1_pieces, g)
-
-        def silu(g):
             nc.scalar.activation(out=silu_gate[g][:], in_=gate[g][:], func=ACT.Silu)
 
         def up_products(g):
@@ -214,12 +214,10 @@ def tile_observationembeddingv2_pa_s_kernel(
             previous = line[i]
             if i in HIDDEN_QUANTISE_STEPS:
                 quantise_hidden(HIDDEN_QUANTISE_STEPS.index(i))
-            if n == 3 and r < PASSES:
-                gate_products(r)
-            if n == 0 and 0 < r <= PASSES:
-                silu(r - 1)
-            if n == 1 and 0 < r <= PASSES:
-                up_products(r - 1)
+            if i in GATE_STEPS:
+                gate_products(GATE_STEPS.index(i))
+            if i in UP_STEPS:
+                up_products(UP_STEPS.index(i))
         quantise(nc, previous)
         shift = broadcast_vectors()
 

from contextlib import ExitStack

import concourse.mybir as mybir
from concourse.masks import make_identity

F32 = mybir.dt.float32
BF16 = mybir.dt.bfloat16
I32 = mybir.dt.int32
U32 = mybir.dt.uint32
U8 = mybir.dt.uint8
FP8X4 = mybir.dt.float8_e4m3fn_x4
ACT = mybir.ActivationFunctionType
ALU = mybir.AluOpType

P = 128
PACK = 4
K_PASS = P * PACK
PAIRS = K_PASS // 2
HID = 1024
D = 512
EPS = 1e-5
CHUNKS = 4
PASSES = HID // K_PASS
GROUPS = ((0, 1), (2,), (3,))
HALF = D // 2
GATE_STEPS = (4, 8)
UP_STEPS = (5, 8)
HIDDEN_STEPS = (7, 10)
HIDDEN_QUANTISE_STEPS = (8, 10)
WARM_PASSES = 11

FLOPS = 2 * P * K_PASS * HID * 2 + 2 * P * HID * D


def new_piece(pool, name, slabs):
    return {
        "slabs": slabs,
        "raw": pool.tile([P, slabs * K_PASS], BF16, name=name + "_raw"),
        "grouped": pool.tile([P, slabs * K_PASS], BF16, name=name + "_grouped", align_bytes=64),
    }


def own_codes(pool, name, piece):
    codes = pool.tile([P, piece["slabs"] * P], U32, name=name + "_codes", align_bytes=64)
    scales = pool.tile([P, piece["slabs"] * P], U8, name=name + "_scales", align_bytes=64)
    piece["codes"] = codes[:]
    piece["scales"] = scales[:]


def flip(nc, banks, piece, identity):
    words = piece["raw"][:].bitcast(F32)
    flipped = banks.tile([P, 2 * PAIRS], F32, name="flipped", tag="flipped")
    for block in range(2 * piece["slabs"]):
        cols = slice(block * P, (block + 1) * P)
        nc.tensor.transpose(flipped[:, cols], words[:, cols], identity[:])
    piece["flipped"] = flipped


def regroup(copy, piece):
    slabs = piece["slabs"]
    copy(
        out=piece["grouped"][:].bitcast(F32).rearrange("p (s i u) -> p s i u", s=slabs, u=2),
        in_=piece["flipped"][:, 0 : slabs * PAIRS].rearrange("p (s u i) -> p s i u", s=slabs, u=2),
    )


def quantise(nc, piece):
    nc.vector.quantize_mx(out=piece["codes"].bitcast(FP8X4), scales=piece["scales"], in_=piece["grouped"][:])


def tile_observationembeddingv2_pa_s_kernel(
    tc, x0, w1_g0, w3_g0, w2_g0, norm_w, norm_b, term_embed0, out
):
    nc = tc.nc
    with ExitStack() as ctx:
        keep = ctx.enter_context(tc.tile_pool(name="keep", bufs=1))
        flip_banks = ctx.enter_context(tc.psum_pool(name="flip_banks", bufs=6))
        sum_banks = ctx.enter_context(tc.psum_pool(name="sum_banks", bufs=1))
        ctx.enter_context(tc.manual_schedule())

        neg_half = keep.tile([P, 1], F32, name="neg_half")
        nc.gpsimd.memset(neg_half[:], -0.5)
        warm = keep.tile([P, 1], F32, name="warm")
        nc.scalar.activation(out=warm[:], in_=neg_half[:], func=ACT.Silu)
        identity = keep.tile([P, P], F32, name="identity")
        make_identity(nc, identity[:])

        x_piece = new_piece(keep, "x", 1)
        w1_pieces = [new_piece(keep, "w1_%d" % c, 2) for c in range(CHUNKS)]
        w3_pieces = [new_piece(keep, "w3_%d" % c, 2) for c in range(CHUNKS)]
        w2_pieces = [new_piece(keep, "w2_%d" % d, PASSES) for d in range(CHUNKS - 1)]
        w2_pieces += [new_piece(keep, "w2_last_%d" % g, 1) for g in range(PASSES)]
        nc.sync.dma_start(out=x_piece["raw"][:], in_=x0)
        w1_rows = w1_g0.rearrange("(c i e) k -> c i (e k)", i=P, e=2)
        w3_rows = w3_g0.rearrange("(c i e) k -> c i (e k)", i=P, e=2)
        rows = keep.tile([P, 2 * D], BF16, name="rows")
        for g in range(PASSES):
            for pieces, rows_in_hbm in ((w1_pieces, w1_rows), (w3_pieces, w3_rows)):
                for c in (2 * g, 2 * g + 1):
                    nc.sync.dma_start(out=pieces[c]["raw"][:], in_=rows_in_hbm[c])
        w2_rows = w2_g0.rearrange("(d i) k -> d i k", i=P)
        for d in range(CHUNKS - 1):
            nc.sync.dma_start(out=w2_pieces[d]["raw"][:], in_=w2_rows[d])
        for g in range(PASSES):
            nc.sync.dma_start(
                out=w2_pieces[CHUNKS - 1 + g]["raw"][:], in_=w2_rows[CHUNKS - 1][:, g * K_PASS : (g + 1) * K_PASS]
            )
        nc.gpsimd.memset(rows[:].bitcast(F32), 0.0)
        nc.sync.dma_start(out=rows[0:1, 0:D], in_=norm_w.rearrange("(o d) -> o d", o=1))
        nc.sync.dma_start(out=rows[0:1, D : 2 * D], in_=norm_b.rearrange("(o d) -> o d", o=1))
        nc.sync.dma_start(out=rows[1:2, D : 2 * D], in_=term_embed0.rearrange("(o d) -> o d", o=1))

        own_codes(keep, "x", x_piece)
        for c in range(CHUNKS):
            own_codes(keep, "w1_%d" % c, w1_pieces[c])
            own_codes(keep, "w3_%d" % c, w3_pieces[c])
        w2_words = []
        for n in range(len(w2_pieces)):
            own_codes(keep, "w2_%d" % n, w2_pieces[n])
        for d in range(CHUNKS - 1):
            codes, scales = w2_pieces[d]["codes"], w2_pieces[d]["scales"]
            w2_words.append([(codes[:, g * P : (g + 1) * P], scales[:, g * P : (g + 1) * P]) for g in range(PASSES)])
        w2_words.append([(piece["codes"], piece["scales"]) for piece in w2_pieces[CHUNKS - 1 :]])

        idle = {"slabs": 1, "grouped": keep.tile([P, K_PASS], BF16, name="idle_grouped", align_bytes=64)}
        own_codes(keep, "idle", idle)
        nc.vector.memset(idle["grouped"][:].bitcast(I32), 0)
        quantise(nc, idle)
        idle_bank = flip_banks.tile([P, P], F32, name="idle_bank", tag="flipped")
        for w in range(WARM_PASSES):
            nc.tensor.matmul_mx(
                out=idle_bank[:],
                lhsT=idle["codes"].bitcast(FP8X4),
                lhsT_scale=idle["scales"],
                rhs=idle["codes"].bitcast(FP8X4),
                rhs_scale=idle["scales"],
                start=True,
                stop=True,
            )

        ones = keep.tile([P, P], BF16, name="ones")
        nc.vector.memset(ones[:], 1.0)

        gain = keep.tile([P, D], F32, name="gain")

        def broadcast_vectors():
            shift = flip_banks.tile([P, D], F32, name="shift", tag="flipped")
            gain_bank = flip_banks.tile([P, D], F32, name="gain_bank", tag="flipped")
            nc.tensor.matmul(out=gain_bank[:], lhsT=ones[:], rhs=rows[:, 0:D], start=True, stop=True)
            nc.tensor.matmul(out=shift[:], lhsT=ones[:], rhs=rows[:, D : 2 * D], start=True, stop=True)
            nc.vector.tensor_copy(out=gain[:], in_=gain_bank[:])
            return shift

        gate = [None] * PASSES
        up = [None] * PASSES
        silu_gate = [keep.tile([P, PACK, P], F32, name="silu_gate_%d" % g) for g in range(PASSES)]
        h_grouped = [keep.tile([P, P, PACK], BF16, name="h_grouped_%d" % g, align_bytes=64) for g in range(PASSES)]
        h_codes = [keep.tile([P, P], U32, name="h_codes_%d" % g, align_bytes=64) for g in range(PASSES)]
        h_scales = [keep.tile([P, P], U8, name="h_scales_%d" % g, align_bytes=64) for g in range(PASSES)]

        def products(bank, pieces, g):
            for u in range(2):
                for e in range(2):
                    nc.tensor.matmul_mx(
                        out=bank[:, 2 * u + e, :],
                        lhsT=pieces[2 * g + u]["codes"][:, e * P : (e + 1) * P].bitcast(FP8X4),
                        lhsT_scale=pieces[2 * g + u]["scales"][:, e * P : (e + 1) * P],
                        rhs=x_piece["codes"].bitcast(FP8X4),
                        rhs_scale=x_piece["scales"],
                        start=True,
                        stop=True,
                    )

        def gate_products(g):
            gate[g] = sum_banks.tile([P, PACK, P], F32, name="gate_%d" % g, tag="left")
            products(gate[g], w1_pieces, g)
            nc.scalar.activation(out=silu_gate[g][:], in_=gate[g][:], func=ACT.Silu)

        def up_products(g):
            up[g] = sum_banks.tile([P, PACK, P], F32, name="up_%d" % g, tag="right")
            products(up[g], w3_pieces, g)

        def hidden(g):
            nc.vector.tensor_tensor(
                out=h_grouped[g][:],
                in0=silu_gate[g][:].rearrange("p t b -> p b t"),
                in1=up[g][:].rearrange("p t b -> p b t"),
                op=ALU.mult,
            )

        def quantise_hidden(g):
            nc.vector.quantize_mx(
                out=h_codes[g][:].bitcast(FP8X4),
                scales=h_scales[g][:],
                in_=h_grouped[g][:].rearrange("p b t -> p (b t)"),
            )

        line = []
        for g in range(PASSES):
            line += w1_pieces[2 * g : 2 * g + 2] + w3_pieces[2 * g : 2 * g + 2]
        line += w2_pieces
        flip(nc, flip_banks, x_piece, identity)
        regroup(nc.scalar.copy, x_piece)
        flip(nc, flip_banks, line[0], identity)
        previous = x_piece
        for i in range(len(line)):
            r, n = divmod(i, CHUNKS)
            if i + 1 < len(line):
                flip(nc, flip_banks, line[i + 1], identity)
            regroup(nc.vector.tensor_copy if (r < PASSES and n == 1) else nc.scalar.copy, line[i])
            if i in HIDDEN_STEPS:
                hidden(HIDDEN_STEPS.index(i))
            quantise(nc, previous)
            previous = line[i]
            if i in HIDDEN_QUANTISE_STEPS:
                quantise_hidden(HIDDEN_QUANTISE_STEPS.index(i))
            if i in GATE_STEPS:
                gate_products(GATE_STEPS.index(i))
            if i in UP_STEPS:
                up_products(UP_STEPS.index(i))
        quantise(nc, previous)
        shift = broadcast_vectors()

        mean_sq = [keep.tile([P, 1], F32, name="mean_sq_%d" % j) for j in range(len(GROUPS))]
        scaled = keep.tile([P, D], F32, name="scaled")
        partial = keep.tile([P, 1], F32, name="partial")
        mean_eps = keep.tile([P, 1], F32, name="mean_eps")
        inv_rms = keep.tile([P, 1], F32, name="inv_rms")
        toks = []
        for j, chunks in enumerate(GROUPS):
            width = len(chunks) * P
            if j < 2:
                tok = sum_banks.tile([P, width], F32, name="tok_%d" % j, tag=("left", "right")[j])
            else:
                tok = flip_banks.tile([P, width], F32, name="tok_%d" % j, tag="flipped")
            toks.append(tok)
            for n, d in enumerate(chunks):
                for g in range(PASSES):
                    codes, scales = w2_words[d][g]
                    nc.tensor.matmul_mx(
                        out=tok[:, n * P : (n + 1) * P],
                        lhsT=h_codes[g][:].bitcast(FP8X4),
                        lhsT_scale=h_scales[g][:],
                        rhs=codes.bitcast(FP8X4),
                        rhs_scale=scales,
                        start=(g == 0),
                        stop=(g == PASSES - 1),
                    )
            squares = keep.tile([P, width], F32, name="squares_%d" % j)
            nc.scalar.activation(
                out=squares[:], in_=tok[:], func=ACT.Square, scale=D**-0.5, accum_out=mean_sq[j][:]
            )
        nc.vector.tensor_scalar(out=partial[:], in0=mean_sq[0][:], scalar1=EPS, scalar2=None, op0=ALU.add)
        nc.vector.scalar_tensor_tensor(
            out=mean_eps[:],
            in0=mean_sq[2][:],
            scalar=mean_sq[1][:, 0:1],
            in1=partial[:],
            op0=ALU.add,
            op1=ALU.add,
        )
        nc.gpsimd.tensor_tensor(out=inv_rms[:], in0=mean_eps[:], in1=neg_half[:], op=ALU.pow)
        first = 0
        for j, chunks in enumerate(GROUPS):
            cols = slice(first, first + len(chunks) * P)
            nc.vector.tensor_tensor(out=scaled[:, cols], in0=toks[j][:], in1=gain[:, cols], op=ALU.mult)
            first += len(chunks) * P

        for j in range(2):
            cols = slice(j * HALF, (j + 1) * HALF)
            result = keep.tile([P, HALF], F32, name="result_%d" % j)
            nc.vector.scalar_tensor_tensor(
                out=result[:],
                in0=scaled[:, cols],
                scalar=inv_rms[:, 0:1],
                in1=shift[:, cols],
                op0=ALU.mult,
                op1=ALU.add,
            )
            nc.sync.dma_start(out=out[:, cols], in_=result[:])
